import numpy as np
import ml_dtypes


def mxq(x, axis, fmt="e4m3"):
    dtype, down = {"e4m3": (ml_dtypes.float8_e4m3fn, 7), "e5m2": (ml_dtypes.float8_e5m2, 14)}[fmt]
    v = np.moveaxis(np.asarray(x, np.float32).astype(ml_dtypes.bfloat16).astype(np.float64), axis, -1)
    blocks = v.reshape(v.shape[:-1] + (-1, 32))
    amax = np.abs(blocks).max(-1, keepdims=True)
    byte = np.maximum(np.where(amax > 0, np.frexp(amax)[1] - 1 + 127, 0) - down, 1)
    scale = np.exp2(byte - 127.0)
    codes = (blocks / scale).astype(np.float32).astype(dtype).astype(np.float64)
    return np.moveaxis((codes * scale).reshape(v.shape), -1, axis)


WIDE = False


def mx_kscale(k):
    if not WIDE:
        return np.ones(k)
    levels = np.array([10, -10, 5, -5, 0])
    a = np.random.permutation(np.resize(levels, k // 512 * 4)).reshape(k // 512, 4)
    idx = np.arange(k)
    return np.exp2(a[idx // 512, idx % 128 // 32])


BF16 = ml_dtypes.bfloat16


def bf(x):
    return np.asarray(x, np.float32).astype(BF16)


def f64(x):
    return np.asarray(x).astype(np.float64)


B, T, D, DV = 1, 2048, 128, 256


def sigmoid(u):
    return 1.0 / (1.0 + np.exp(-u))


def setup_inputs():
    s = mx_kscale(T)
    q = np.random.standard_normal((B, T, D)) * 1.6
    k = np.random.standard_normal((B, T, D)) * 1.6
    q[..., 0] = 4.0
    q[..., 1] = -4.0
    k[..., 0] += np.log(s)[None, :] * np.sqrt(D) / 4.0
    v = np.random.standard_normal((B, T, DV)) * s[None, :, None] * np.mean(1.0 / s)
    return {"q": bf(q),
            "k": bf(k),
            "v": bf(v),
            "mask": (np.random.random((1, T, T)) < 0.7).astype(np.int32),
            "mode": bf(0.5 + 0.3 * np.random.standard_normal(1))}


def reference(q, k, v, mask, mode):
    q, k, v = f64(q), f64(k), f64(v)
    scale = D ** (-0.5)
    meson = -(q @ k.transpose(0, 2, 1)) * scale
    k_perm = np.roll(k, 1, axis=-1)
    baryon = (q @ k_perm.transpose(0, 2, 1)) * scale
    alpha = sigmoid(f64(mode))
    attn = alpha * meson + (1.0 - alpha) * baryon
    attn = np.where(f64(mask) == 0.0, -np.inf, attn)
    e = np.exp(attn - attn.max(-1, keepdims=True))
    return (mxq(e, 2, "e4m3") @ mxq(v, 1, "e4m3")) / e.sum(-1, keepdims=True)

@@ -1,0 +1,230 @@
+import math
+
+import concourse.mybir as mybir
+from concourse.masks import make_identity
+
+F32 = mybir.dt.float32
+BF16 = mybir.dt.bfloat16
+I32 = mybir.dt.int32
+U32 = mybir.dt.uint32
+U8 = mybir.dt.uint8
+FP8X4 = mybir.dt.float8_e4m3fn_x4
+ALU = mybir.AluOpType
+ACT = mybir.ActivationFunctionType
+
+P = 128
+T = 2048
+D = 128
+DV = 256
+PACK = 4
+K_PASS = P * PACK
+N_PASS = T // K_PASS
+N_TILES = T // P
+BANK = 512
+N_BANKS = T // BANK
+GROUP = 4
+MASKS_AHEAD = 3
+
+SHRINK = 2.0 ** -40
+GROW = 2.0 ** 40
+
+FLOPS = 2 * (2 * T * T * D) + 2 * T * T * DV
+
+
+def tile_dualmodehead_kernel(tc, q, k, v, mask, mode, out):
+    nc = tc.nc
+    q_rows = q.flatten_outer_dims().rearrange("(p n) d -> p n d", n=N_TILES)
+    k_rows = k.flatten_outer_dims().rearrange("(j p) d -> p j d", p=P)
+    v_rows = v.flatten_outer_dims().rearrange("(g p) w -> p g w", p=P)
+    mask_tiles = mask.bitcast(I32).flatten_outer_dims().rearrange("(p n) (k w) -> n p k w", n=N_TILES, w=2)
+    out_tiles = out.flatten_outer_dims().rearrange("(p n) w -> n p w", n=N_TILES)
+
+    with tc.tile_pool(name="keep", bufs=1) as keep, \
+            tc.tile_pool(name="prep", bufs=2) as prep, \
+            tc.tile_pool(name="mask_pool", bufs=MASKS_AHEAD + 1) as mask_pool, \
+            tc.tile_pool(name="work", bufs=3) as work, \
+            tc.tile_pool(name="small", bufs=6) as small, \
+            tc.psum_pool(name="score_psum", bufs=N_BANKS) as score_psum, \
+            tc.psum_pool(name="turn_psum", bufs=3) as turn_psum, \
+            tc.psum_pool(name="out_psum", bufs=1) as out_psum, \
+            tc.manual_schedule():
+
+        mask_of, score_of, shifted_of, neg_max_of, row_sum_of = {}, {}, {}, {}, {}
+        e_of, turned_of, grouped_of, codes_of, scales_of, acc_of = {}, {}, {}, {}, {}, {}
+
+        def load_mask(n):
+            if not 0 <= n < N_TILES:
+                return
+            mask_of[n] = mask_pool.tile([P, T, 2], I32, name="mask_sb")
+            nc.sync.dma_start(out=mask_of[n][:], in_=mask_tiles[n])
+
+        mode_sb = keep.tile([P, 1], BF16)
+        nc.sync.dma_start(out=mode_sb[:], in_=mode.partition_broadcast(P))
+        q_ext = keep.tile([P, N_TILES, D + 1], BF16)
+        nc.sync.dma_start(out=q_ext[:, :, 0:D], in_=q_rows)
+        k_sb = keep.tile([P, N_TILES, D], BF16)
+        nc.sync.dma_start(out=k_sb[:], in_=k_rows)
+        load_mask(0)
+        v_raw = keep.tile([P, N_PASS, PACK, DV], BF16)
+        nc.sync.dma_start(out=v_raw[:].rearrange("p c t w -> p (c t) w"), in_=v_rows)
+        load_mask(1)
+
+        ident = keep.tile([P, P], BF16)
+        make_identity(nc, ident[:])
+
+        exp_neg = keep.tile([P, 1], F32)
+        nc.scalar.activation(out=exp_neg[:], in_=mode_sb[:], func=ACT.Exp, scale=-1.0)
+        denom = keep.tile([P, 1], F32)
+        nc.vector.tensor_scalar_add(out=denom[:], in0=exp_neg[:], scalar1=1.0)
+        alpha = keep.tile([P, 1], F32)
+        nc.vector.reciprocal(out=alpha[:], in_=denom[:])
+        unit = SHRINK / math.sqrt(D)
+        w_meson = keep.tile([P, 1], F32)
+        nc.vector.tensor_scalar_mul(out=w_meson[:], in0=alpha[:], scalar1=unit)
+        w_baryon = keep.tile([P, 1], F32)
+        nc.vector.tensor_scalar(out=w_baryon[:], in0=alpha[:], scalar1=-unit, scalar2=unit,
+                                op0=ALU.mult, op1=ALU.add)
+
+        nc.scalar.copy(out=q_ext[:, :, D:D + 1], in_=q_ext[:, :, 0:1])
+        qT = keep.tile([P, N_TILES, 2, P], BF16)
+        kT = keep.tile([P, T], BF16)
+
+        def blend_queries(g):
+            tiles = slice(GROUP * g, GROUP * (g + 1))
+            meson_part = prep.tile([P, GROUP, D], F32)
+            nc.scalar.activation(out=meson_part[:], in_=q_ext[:, tiles, 0:D], func=ACT.Copy,
+                                 scale=w_meson[:, 0:1])
+            blend = prep.tile([P, GROUP, D], F32)
+            nc.vector.scalar_tensor_tensor(out=blend[:], in0=q_ext[:, tiles, 1:D + 1],
+                                           scalar=w_baryon[:, 0:1], in1=meson_part[:],
+                                           op0=ALU.mult, op1=ALU.subtract)
+            high = prep.tile([P, GROUP, D], BF16)
+            nc.vector.tensor_copy(out=high[:], in_=blend[:])
+            low = prep.tile([P, GROUP, D], BF16)
+            nc.gpsimd.tensor_tensor(out=low[:], in0=blend[:], in1=high[:], op=ALU.subtract)
+            turned = turn_psum.tile([P, GROUP, 2, P], BF16, tag="turned")
+            for i in range(GROUP):
+                nc.tensor.transpose(turned[:, i, 0, :], high[:, i, :], ident[:])
+            for i in range(GROUP):
+                nc.tensor.transpose(turned[:, i, 1, :], low[:, i, :], ident[:])
+            nc.scalar.copy(out=qT[:, tiles, :, :], in_=turned[:])
+
+        def turn_keys(h):
+            turned = turn_psum.tile([P, 8, P], BF16, tag="turned")
+            for j in range(8):
+                nc.tensor.transpose(turned[:, j, :], k_sb[:, 8 * h + j, :], ident[:])
+            nc.scalar.copy(out=kT[:, 1024 * h:1024 * (h + 1)], in_=turned[:].rearrange("p j c -> p (j c)"))
+
+        blend_queries(0)
+        turn_keys(0)
+        turn_keys(1)
+        for g in range(1, N_TILES // GROUP):
+            blend_queries(g)
+
+        v_grouped = keep.tile([P, N_PASS, DV, PACK], BF16, align_bytes=64)
+        v_codes = keep.tile([P, N_PASS, DV], U32, align_bytes=64)
+        v_scales = keep.tile([P, N_PASS, DV], U8, align_bytes=64)
+        for c in range(N_PASS):
+            nc.gpsimd.tensor_scalar(out=v_grouped[:, c], in0=v_raw[:, c].rearrange("p t w -> p w t"),
+                                    scalar1=1.0, scalar2=0.0, op0=ALU.mult, op1=ALU.add)
+
+        def quantise_v():
+            nc.vector.quantize_mx(out=v_codes[:].rearrange("p c w -> p (c w)").bitcast(FP8X4),
+                                  scales=v_scales[:].rearrange("p c w -> p (c w)"),
+                                  in_=v_grouped[:].rearrange("p c w t -> p (c w t)"))
+
+        def scores(n, b):
+            if not 0 <= n < N_TILES:
+                return
+            cols = slice(BANK * b, BANK * (b + 1))
+            score_of[n, b] = score_psum.tile([P, BANK], F32, name="score")
+            nc.tensor.matmul(score_of[n, b][:], lhsT=qT[:, n, 0, :], rhs=kT[:, cols], start=True, stop=False)
+            nc.tensor.matmul(score_of[n, b][:], lhsT=qT[:, n, 1, :], rhs=kT[:, cols], start=False, stop=True)
+
+        def mask_scores(n, b):
+            if not 0 <= n < N_TILES:
+                return
+            cols = slice(BANK * b, BANK * (b + 1))
+            if b == 0:
+                shifted_of[n] = work.tile([P, T], F32, name="shifted")
+            nc.vector.scalar_tensor_tensor(out=shifted_of[n][:, cols], in0=mask_of[n][:, cols, 0], scalar=1.0,
+                                           in1=score_of[n, b][:], op0=ALU.subtract, op1=ALU.add)
+
+        def row_max(n):
+            if not 0 <= n < N_TILES:
+                return
+            neg_max_of[n] = small.tile([P, 1], F32, name="neg_max")
+            nc.vector.tensor_scalar(out=shifted_of[n][:], in0=shifted_of[n][:], scalar1=-GROW, scalar2=None,
+                                    op0=ALU.mult, op1=ALU.min, accum_out=neg_max_of[n][:])
+
+        def exponent(n):
+            if not 0 <= n < N_TILES:
+                return
+            e_of[n] = work.tile([P, T], BF16, name="e_sb")
+            row_sum_of[n] = small.tile([P, 1], F32, name="row_sum")
+            nc.scalar.activation(out=e_of[n][:], in_=shifted_of[n][:], func=ACT.Exp, bias=neg_max_of[n][:, 0:1],
+                                 scale=-1.0, accum_out=row_sum_of[n][:])
+
+        def turn(n, c):
+            if not 0 <= n < N_TILES:
+                return
+            if c % 2 == 0:
+                turned_of[n, c // 2] = turn_psum.tile([P, 2, PACK, P], BF16, name="turned")
+            for t in range(PACK):
+                first = K_PASS * c + P * t
+                nc.tensor.transpose(turned_of[n, c // 2][:, c % 2, t, :], e_of[n][:, first:first + P], ident[:])
+
+        def regroup(n):
+            if not 0 <= n < N_TILES:
+                return
+            grouped_of[n] = work.tile([P, N_PASS, P, PACK], BF16, name="grouped", align_bytes=64)
+            for h in range(2):
+                nc.scalar.copy(out=grouped_of[n][:, 2 * h:2 * h + 2],
+                               in_=turned_of[n, h][:].rearrange("p c t r -> p c r t"))
+
+        def quantise(n):
+            if not 0 <= n < N_TILES:
+                return
+            codes_of[n] = work.tile([P, N_PASS, P], U32, name="e_codes", align_bytes=64)
+            scales_of[n] = work.tile([P, N_PASS, P], U8, name="e_scales", align_bytes=64)
+            nc.vector.quantize_mx(out=codes_of[n][:].rearrange("p c r -> p (c r)").bitcast(FP8X4),
+                                  scales=scales_of[n][:].rearrange("p c r -> p (c r)"),
+                                  in_=grouped_of[n][:].rearrange("p c r t -> p (c r t)"))
+
+        def multiply(n):
+            if not 0 <= n < N_TILES:
+                return
+            acc_of[n] = out_psum.tile([P, DV], F32, name="acc")
+            for c in range(N_PASS):
+                nc.tensor.matmul_mx(out=acc_of[n][:], lhsT=codes_of[n][:, c, :].bitcast(FP8X4),
+                                    lhsT_scale=scales_of[n][:, c, :],
+                                    rhs=v_codes[:, c, :].bitcast(FP8X4), rhs_scale=v_scales[:, c, :],
+                                    start=(c == 0), stop=(c == N_PASS - 1))
+
+        def finish(n):
+            if not 0 <= n < N_TILES:
+                return
+            inv_sum = small.tile([P, 1], F32)
+            nc.vector.reciprocal(out=inv_sum[:], in_=row_sum_of[n][:])
+            result = work.tile([P, DV], F32)
+            nc.scalar.activation(out=result[:], in_=acc_of[n][:], func=ACT.Copy, scale=inv_sum[:, 0:1])
+            nc.sync.dma_start(out=out_tiles[n], in_=result[:])
+
+        def step(m):
+            load_mask(m + MASKS_AHEAD)
+            quantise(m - 3)
+            multiply(m - 3)
+            exponent(m - 1)
+            regroup(m - 2)
+            finish(m - 3)
+            for b in range(N_BANKS):
+                mask_scores(m, b)
+                scores(m + 1, b)
+                turn(m - 1, b)
+            row_max(m)
+
+        for m in range(-1, 3):
+            step(m)
+        quantise_v()
+        for m in range(3, N_TILES + 3):
+            step(m)

@@ -23,6 +23,7 @@ N_TILES = T // P
 BANK = 512
 N_BANKS = T // BANK
 GROUP = 4
+N_GROUPS = N_TILES // GROUP
 MASKS_AHEAD = 3
 
 SHRINK = 2.0 ** -40
@@ -40,7 +41,7 @@ def tile_dualmodehead_kernel(tc, q, k, v, mask, mode, out):
     out_tiles = out.flatten_outer_dims().rearrange("(p n) w -> n p w", n=N_TILES)
 
     with tc.tile_pool(name="keep", bufs=1) as keep, \
-            tc.tile_pool(name="prep", bufs=2) as prep, \
+            tc.tile_pool(name="prep", bufs=N_GROUPS) as prep, \
             tc.tile_pool(name="mask_pool", bufs=MASKS_AHEAD + 1) as mask_pool, \
             tc.tile_pool(name="work", bufs=3) as work, \
             tc.tile_pool(name="small", bufs=6) as small, \
@@ -89,24 +90,26 @@ def tile_dualmodehead_kernel(tc, q, k, v, mask, mode, out):
         qT = keep.tile([P, N_TILES, 2, P], BF16)
         kT = keep.tile([P, T], BF16)
 
+        blend_of, high_of, low_of = {}, {}, {}
+
         def blend_queries(g):
             tiles = slice(GROUP * g, GROUP * (g + 1))
-            meson_part = prep.tile([P, GROUP, D], F32)
-            nc.scalar.activation(out=meson_part[:], in_=q_ext[:, tiles, 0:D], func=ACT.Copy,
-                                 scale=w_meson[:, 0:1])
-            blend = prep.tile([P, GROUP, D], F32)
-            nc.vector.scalar_tensor_tensor(out=blend[:], in0=q_ext[:, tiles, 1:D + 1],
-                                           scalar=w_baryon[:, 0:1], in1=meson_part[:],
+            blend_of[g] = prep.tile([P, GROUP, D], F32, name="blend")
+            nc.vector.scalar_tensor_tensor(out=blend_of[g][:], in0=q_ext[:, tiles, 1:D + 1],
+                                           scalar=w_baryon[:, 0:1], in1=meson_of[g][:],
                                            op0=ALU.mult, op1=ALU.subtract)
-            high = prep.tile([P, GROUP, D], BF16)
-            nc.vector.tensor_copy(out=high[:], in_=blend[:])
-            low = prep.tile([P, GROUP, D], BF16)
-            nc.gpsimd.tensor_tensor(out=low[:], in0=blend[:], in1=high[:], op=ALU.subtract)
+            high_of[g] = prep.tile([P, GROUP, D], BF16, name="high")
+            nc.vector.tensor_copy(out=high_of[g][:], in_=blend_of[g][:])
+            low_of[g] = prep.tile([P, GROUP, D], BF16, name="low")
+            nc.gpsimd.tensor_tensor(out=low_of[g][:], in0=blend_of[g][:], in1=high_of[g][:], op=ALU.subtract)
+
+        def turn_queries(g):
+            tiles = slice(GROUP * g, GROUP * (g + 1))
             turned = turn_psum.tile([P, GROUP, 2, P], BF16, tag="turned")
             for i in range(GROUP):
-                nc.tensor.transpose(turned[:, i, 0, :], high[:, i, :], ident[:])
+                nc.tensor.transpose(turned[:, i, 0, :], high_of[g][:, i, :], ident[:])
             for i in range(GROUP):
-                nc.tensor.transpose(turned[:, i, 1, :], low[:, i, :], ident[:])
+                nc.tensor.transpose(turned[:, i, 1, :], low_of[g][:, i, :], ident[:])
             nc.scalar.copy(out=qT[:, tiles, :, :], in_=turned[:])
 
         def turn_keys(h):
@@ -115,10 +118,12 @@ def tile_dualmodehead_kernel(tc, q, k, v, mask, mode, out):
                 nc.tensor.transpose(turned[:, j, :], k_sb[:, 8 * h + j, :], ident[:])
             nc.scalar.copy(out=kT[:, 1024 * h:1024 * (h + 1)], in_=turned[:].rearrange("p j c -> p (j c)"))
 
-        blend_queries(0)
-        turn_keys(0)
-        turn_keys(1)
-        for g in range(1, N_TILES // GROUP):
+        meson_of = {}
+        for g in range(N_GROUPS):
+            meson_of[g] = prep.tile([P, GROUP, D], F32, name="meson_part")
+            nc.scalar.activation(out=meson_of[g][:], in_=q_ext[:, GROUP * g:GROUP * (g + 1), 0:D], func=ACT.Copy,
+                                 scale=w_meson[:, 0:1])
+        for g in range(N_GROUPS):
             blend_queries(g)
 
         v_grouped = keep.tile([P, N_PASS, DV, PACK], BF16, align_bytes=64)
@@ -212,18 +217,25 @@ def tile_dualmodehead_kernel(tc, q, k, v, mask, mode, out):
 
         def step(m):
             load_mask(m + MASKS_AHEAD)
-            quantise(m - 3)
-            multiply(m - 3)
             exponent(m - 1)
             regroup(m - 2)
-            finish(m - 3)
             for b in range(N_BANKS):
                 mask_scores(m, b)
                 scores(m + 1, b)
-                turn(m - 1, b)
+            quantise(m - 3)
+            multiply(m - 3)
+            finish(m - 3)
+            for c in range(N_PASS):
+                turn(m - 1, c)
             row_max(m)
 
-        for m in range(-1, 3):
+        turn_keys(0)
+        turn_keys(1)
+        turn_queries(0)
+        step(-1)
+        for g in range(1, N_GROUPS):
+            turn_queries(g)
+        for m in range(0, 3):
             step(m)
         quantise_v()
         for m in range(3, N_TILES + 3):

@@ -22,7 +22,7 @@ N_PASS = T // K_PASS
 N_TILES = T // P
 BANK = 512
 N_BANKS = T // BANK
-GROUP = 4
+GROUP = 2
 N_GROUPS = N_TILES // GROUP
 MASKS_AHEAD = 3
 
@@ -51,13 +51,15 @@ def tile_dualmodehead_kernel(tc, q, k, v, mask, mode, out):
             tc.manual_schedule():
 
         mask_of, score_of, shifted_of, neg_max_of, row_sum_of = {}, {}, {}, {}, {}
-        e_of, turned_of, grouped_of, codes_of, scales_of, acc_of = {}, {}, {}, {}, {}, {}
+        e_of, turned_of, grouped_of, codes_of, scales_of, acc_of, inv_sum_of = {}, {}, {}, {}, {}, {}, {}
 
         def load_mask(n):
             if not 0 <= n < N_TILES:
                 return
             mask_of[n] = mask_pool.tile([P, T, 2], I32, name="mask_sb")
-            nc.sync.dma_start(out=mask_of[n][:], in_=mask_tiles[n])
+            for h in range(2):
+                keys = slice(T // 2 * h, T // 2 * (h + 1))
+                nc.sync.dma_start(out=mask_of[n][:, keys, :], in_=mask_tiles[n][:, keys, :])
 
         mode_sb = keep.tile([P, 1], BF16)
         nc.sync.dma_start(out=mode_sb[:], in_=mode.partition_broadcast(P))
@@ -72,6 +74,8 @@ def tile_dualmodehead_kernel(tc, q, k, v, mask, mode, out):
 
         ident = keep.tile([P, P], BF16)
         make_identity(nc, ident[:])
+        minus_one = keep.tile([P, 1], F32)
+        nc.gpsimd.memset(minus_one[:], -1.0)
 
         exp_neg = keep.tile([P, 1], F32)
         nc.scalar.activation(out=exp_neg[:], in_=mode_sb[:], func=ACT.Exp, scale=-1.0)
@@ -99,7 +103,9 @@ def tile_dualmodehead_kernel(tc, q, k, v, mask, mode, out):
                                            scalar=w_baryon[:, 0:1], in1=meson_of[g][:],
                                            op0=ALU.mult, op1=ALU.subtract)
             high_of[g] = prep.tile([P, GROUP, D], BF16, name="high")
-            nc.vector.tensor_copy(out=high_of[g][:], in_=blend_of[g][:])
+            nc.vector.scalar_tensor_tensor(out=high_of[g][:], in0=q_ext[:, tiles, 1:D + 1],
+                                           scalar=w_baryon[:, 0:1], in1=meson_of[g][:],
+                                           op0=ALU.mult, op1=ALU.subtract)
             low_of[g] = prep.tile([P, GROUP, D], BF16, name="low")
             nc.gpsimd.tensor_tensor(out=low_of[g][:], in0=blend_of[g][:], in1=high_of[g][:], op=ALU.subtract)
 
@@ -169,6 +175,8 @@ def tile_dualmodehead_kernel(tc, q, k, v, mask, mode, out):
             row_sum_of[n] = small.tile([P, 1], F32, name="row_sum")
             nc.scalar.activation(out=e_of[n][:], in_=shifted_of[n][:], func=ACT.Exp, bias=neg_max_of[n][:, 0:1],
                                  scale=-1.0, accum_out=row_sum_of[n][:])
+            inv_sum_of[n] = small.tile([P, 1], F32, name="inv_sum")
+            nc.gpsimd.tensor_tensor(out=inv_sum_of[n][:], in0=row_sum_of[n][:], in1=minus_one[:], op=ALU.pow)
 
         def turn(n, c):
             if not 0 <= n < N_TILES:
@@ -179,13 +187,16 @@ def tile_dualmodehead_kernel(tc, q, k, v, mask, mode, out):
                 first = K_PASS * c + P * t
                 nc.tensor.transpose(turned_of[n, c // 2][:, c % 2, t, :], e_of[n][:, first:first + P], ident[:])
 
-        def regroup(n):
+        def regroup(n, h, on_vector):
             if not 0 <= n < N_TILES:
                 return
-            grouped_of[n] = work.tile([P, N_PASS, P, PACK], BF16, name="grouped", align_bytes=64)
-            for h in range(2):
-                nc.scalar.copy(out=grouped_of[n][:, 2 * h:2 * h + 2],
-                               in_=turned_of[n, h][:].rearrange("p c t r -> p c r t"))
+            if h == 0:
+                grouped_of[n] = work.tile([P, N_PASS, P, PACK], BF16, name="grouped", align_bytes=64)
+            side_by_side = turned_of[n, h][:].rearrange("p c t r -> p c r t")
+            if on_vector:
+                nc.vector.tensor_copy(out=grouped_of[n][:, 2 * h:2 * h + 2], in_=side_by_side)
+            else:
+                nc.scalar.copy(out=grouped_of[n][:, 2 * h:2 * h + 2], in_=side_by_side)
 
         def quantise(n):
             if not 0 <= n < N_TILES:
@@ -209,16 +220,15 @@ def tile_dualmodehead_kernel(tc, q, k, v, mask, mode, out):
         def finish(n):
             if not 0 <= n < N_TILES:
                 return
-            inv_sum = small.tile([P, 1], F32)
-            nc.vector.reciprocal(out=inv_sum[:], in_=row_sum_of[n][:])
             result = work.tile([P, DV], F32)
-            nc.scalar.activation(out=result[:], in_=acc_of[n][:], func=ACT.Copy, scale=inv_sum[:, 0:1])
+            nc.scalar.activation(out=result[:], in_=acc_of[n][:], func=ACT.Copy, scale=inv_sum_of[n][:, 0:1])
             nc.sync.dma_start(out=out_tiles[n], in_=result[:])
 
         def step(m):
             load_mask(m + MASKS_AHEAD)
             exponent(m - 1)
-            regroup(m - 2)
+            regroup(m - 2, 0, False)
+            regroup(m - 2, 1, False)
             for b in range(N_BANKS):
                 mask_scores(m, b)
                 scores(m + 1, b)
@@ -238,5 +248,23 @@ def tile_dualmodehead_kernel(tc, q, k, v, mask, mode, out):
         for m in range(0, 3):
             step(m)
         quantise_v()
-        for m in range(3, N_TILES + 3):
+        for m in range(3, N_TILES):
             step(m)
+
+        last = N_TILES - 1
+        exponent(last)
+        quantise(last - 2)
+        multiply(last - 2)
+        finish(last - 2)
+        regroup(last - 1, 0, True)
+        regroup(last - 1, 1, True)
+        for c in range(N_PASS):
+            turn(last, c)
+        quantise(last - 1)
+        multiply(last - 1)
+        regroup(last, 0, False)
+        regroup(last, 1, True)
+        finish(last - 1)
+        quantise(last)
+        multiply(last)
+        finish(last)

@@ -50,7 +50,7 @@ def tile_dualmodehead_kernel(tc, q, k, v, mask, mode, out):
             tc.psum_pool(name="out_psum", bufs=1) as out_psum, \
             tc.manual_schedule():
 
-        mask_of, score_of, shifted_of, neg_max_of, row_sum_of = {}, {}, {}, {}, {}
+        mask_of, score_of, shifted_of, row_max_of, row_sum_of = {}, {}, {}, {}, {}
         e_of, turned_of, grouped_of, codes_of, scales_of, acc_of, inv_sum_of = {}, {}, {}, {}, {}, {}, {}
 
         def load_mask(n):
@@ -164,17 +164,18 @@ def tile_dualmodehead_kernel(tc, q, k, v, mask, mode, out):
         def row_max(n):
             if not 0 <= n < N_TILES:
                 return
-            neg_max_of[n] = small.tile([P, 1], F32, name="neg_max")
-            nc.vector.tensor_scalar(out=shifted_of[n][:], in0=shifted_of[n][:], scalar1=-GROW, scalar2=None,
-                                    op0=ALU.mult, op1=ALU.min, accum_out=neg_max_of[n][:])
+            row_max_of[n] = small.tile([P, 1], F32, name="row_max")
+            nc.vector.tensor_reduce(out=row_max_of[n][:], in_=shifted_of[n][:], axis=mybir.AxisListType.X, op=ALU.max)
 
         def exponent(n):
             if not 0 <= n < N_TILES:
                 return
+            neg_max = small.tile([P, 1], F32)
+            nc.scalar.mul(out=neg_max[:], in_=row_max_of[n][:], mul=-GROW)
             e_of[n] = work.tile([P, T], BF16, name="e_sb")
             row_sum_of[n] = small.tile([P, 1], F32, name="row_sum")
-            nc.scalar.activation(out=e_of[n][:], in_=shifted_of[n][:], func=ACT.Exp, bias=neg_max_of[n][:, 0:1],
-                                 scale=-1.0, accum_out=row_sum_of[n][:])
+            nc.scalar.activation(out=e_of[n][:], in_=shifted_of[n][:], func=ACT.Exp, bias=neg_max[:, 0:1],
+                                 scale=GROW, accum_out=row_sum_of[n][:])
             inv_sum_of[n] = small.tile([P, 1], F32, name="inv_sum")
             nc.gpsimd.tensor_tensor(out=inv_sum_of[n][:], in0=row_sum_of[n][:], in1=minus_one[:], op=ALU.pow)
 

import math

import concourse.mybir as mybir
from concourse.masks import make_identity

F32 = mybir.dt.float32
BF16 = mybir.dt.bfloat16
I32 = mybir.dt.int32
U32 = mybir.dt.uint32
U8 = mybir.dt.uint8
FP8X4 = mybir.dt.float8_e4m3fn_x4
ALU = mybir.AluOpType
ACT = mybir.ActivationFunctionType

P = 128
T = 2048
D = 128
DV = 256
PACK = 4
K_PASS = P * PACK
N_PASS = T // K_PASS
N_TILES = T // P
BANK = 512
N_BANKS = T // BANK
GROUP = 2
N_GROUPS = N_TILES // GROUP
MASKS_AHEAD = 3

SHRINK = 2.0 ** -40
GROW = 2.0 ** 40

FLOPS = 2 * (2 * T * T * D) + 2 * T * T * DV


def tile_dualmodehead_kernel(tc, q, k, v, mask, mode, out):
    nc = tc.nc
    q_rows = q.flatten_outer_dims().rearrange("(p n) d -> p n d", n=N_TILES)
    k_rows = k.flatten_outer_dims().rearrange("(j p) d -> p j d", p=P)
    v_rows = v.flatten_outer_dims().rearrange("(g p) w -> p g w", p=P)
    mask_tiles = mask.bitcast(I32).flatten_outer_dims().rearrange("(p n) (k w) -> n p k w", n=N_TILES, w=2)
    out_tiles = out.flatten_outer_dims().rearrange("(p n) w -> n p w", n=N_TILES)

    with tc.tile_pool(name="keep", bufs=1) as keep, \
            tc.tile_pool(name="prep", bufs=N_GROUPS) as prep, \
            tc.tile_pool(name="mask_pool", bufs=MASKS_AHEAD + 1) as mask_pool, \
            tc.tile_pool(name="work", bufs=3) as work, \
            tc.tile_pool(name="small", bufs=6) as small, \
            tc.psum_pool(name="score_psum", bufs=N_BANKS) as score_psum, \
            tc.psum_pool(name="turn_psum", bufs=3) as turn_psum, \
            tc.psum_pool(name="out_psum", bufs=1) as out_psum, \
            tc.manual_schedule():

        mask_of, score_of, shifted_of, row_max_of, row_sum_of = {}, {}, {}, {}, {}
        e_of, turned_of, grouped_of, codes_of, scales_of, acc_of, inv_sum_of = {}, {}, {}, {}, {}, {}, {}

        def load_mask(n):
            if not 0 <= n < N_TILES:
                return
            mask_of[n] = mask_pool.tile([P, T, 2], I32, name="mask_sb")
            for h in range(2):
                keys = slice(T // 2 * h, T // 2 * (h + 1))
                nc.sync.dma_start(out=mask_of[n][:, keys, :], in_=mask_tiles[n][:, keys, :])

        mode_sb = keep.tile([P, 1], BF16)
        nc.sync.dma_start(out=mode_sb[:], in_=mode.partition_broadcast(P))
        q_ext = keep.tile([P, N_TILES, D + 1], BF16)
        nc.sync.dma_start(out=q_ext[:, :, 0:D], in_=q_rows)
        k_sb = keep.tile([P, N_TILES, D], BF16)
        nc.sync.dma_start(out=k_sb[:], in_=k_rows)
        load_mask(0)
        v_raw = keep.tile([P, N_PASS, PACK, DV], BF16)
        nc.sync.dma_start(out=v_raw[:].rearrange("p c t w -> p (c t) w"), in_=v_rows)
        load_mask(1)

        ident = keep.tile([P, P], BF16)
        make_identity(nc, ident[:])
        minus_one = keep.tile([P, 1], F32)
        nc.gpsimd.memset(minus_one[:], -1.0)

        exp_neg = keep.tile([P, 1], F32)
        nc.scalar.activation(out=exp_neg[:], in_=mode_sb[:], func=ACT.Exp, scale=-1.0)
        denom = keep.tile([P, 1], F32)
        nc.vector.tensor_scalar_add(out=denom[:], in0=exp_neg[:], scalar1=1.0)
        alpha = keep.tile([P, 1], F32)
        nc.vector.reciprocal(out=alpha[:], in_=denom[:])
        unit = SHRINK / math.sqrt(D)
        w_meson = keep.tile([P, 1], F32)
        nc.vector.tensor_scalar_mul(out=w_meson[:], in0=alpha[:], scalar1=unit)
        w_baryon = keep.tile([P, 1], F32)
        nc.vector.tensor_scalar(out=w_baryon[:], in0=alpha[:], scalar1=-unit, scalar2=unit,
                                op0=ALU.mult, op1=ALU.add)

        nc.scalar.copy(out=q_ext[:, :, D:D + 1], in_=q_ext[:, :, 0:1])
        qT = keep.tile([P, N_TILES, 2, P], BF16)
        kT = keep.tile([P, T], BF16)

        blend_of, high_of, low_of = {}, {}, {}

        def blend_queries(g):
            tiles = slice(GROUP * g, GROUP * (g + 1))
            blend_of[g] = prep.tile([P, GROUP, D], F32, name="blend")
            nc.vector.scalar_tensor_tensor(out=blend_of[g][:], in0=q_ext[:, tiles, 1:D + 1],
                                           scalar=w_baryon[:, 0:1], in1=meson_of[g][:],
                                           op0=ALU.mult, op1=ALU.subtract)
            high_of[g] = prep.tile([P, GROUP, D], BF16, name="high")
            nc.vector.scalar_tensor_tensor(out=high_of[g][:], in0=q_ext[:, tiles, 1:D + 1],
                                           scalar=w_baryon[:, 0:1], in1=meson_of[g][:],
                                           op0=ALU.mult, op1=ALU.subtract)
            low_of[g] = prep.tile([P, GROUP, D], BF16, name="low")
            nc.gpsimd.tensor_tensor(out=low_of[g][:], in0=blend_of[g][:], in1=high_of[g][:], op=ALU.subtract)

        def turn_queries(g):
            tiles = slice(GROUP * g, GROUP * (g + 1))
            turned = turn_psum.tile([P, GROUP, 2, P], BF16, tag="turned")
            for i in range(GROUP):
                nc.tensor.transpose(turned[:, i, 0, :], high_of[g][:, i, :], ident[:])
            for i in range(GROUP):
                nc.tensor.transpose(turned[:, i, 1, :], low_of[g][:, i, :], ident[:])
            nc.scalar.copy(out=qT[:, tiles, :, :], in_=turned[:])

        def turn_keys(h):
            turned = turn_psum.tile([P, 8, P], BF16, tag="turned")
            for j in range(8):
                nc.tensor.transpose(turned[:, j, :], k_sb[:, 8 * h + j, :], ident[:])
            nc.scalar.copy(out=kT[:, 1024 * h:1024 * (h + 1)], in_=turned[:].rearrange("p j c -> p (j c)"))

        meson_of = {}
        for g in range(N_GROUPS):
            meson_of[g] = prep.tile([P, GROUP, D], F32, name="meson_part")
            nc.scalar.activation(out=meson_of[g][:], in_=q_ext[:, GROUP * g:GROUP * (g + 1), 0:D], func=ACT.Copy,
                                 scale=w_meson[:, 0:1])
        for g in range(N_GROUPS):
            blend_queries(g)

        v_grouped = keep.tile([P, N_PASS, DV, PACK], BF16, align_bytes=64)
        v_codes = keep.tile([P, N_PASS, DV], U32, align_bytes=64)
        v_scales = keep.tile([P, N_PASS, DV], U8, align_bytes=64)
        for c in range(N_PASS):
            nc.gpsimd.tensor_scalar(out=v_grouped[:, c], in0=v_raw[:, c].rearrange("p t w -> p w t"),
                                    scalar1=1.0, scalar2=0.0, op0=ALU.mult, op1=ALU.add)

        def quantise_v():
            nc.vector.quantize_mx(out=v_codes[:].rearrange("p c w -> p (c w)").bitcast(FP8X4),
                                  scales=v_scales[:].rearrange("p c w -> p (c w)"),
                                  in_=v_grouped[:].rearrange("p c w t -> p (c w t)"))

        def scores(n, b):
            if not 0 <= n < N_TILES:
                return
            cols = slice(BANK * b, BANK * (b + 1))
            score_of[n, b] = score_psum.tile([P, BANK], F32, name="score")
            nc.tensor.matmul(score_of[n, b][:], lhsT=qT[:, n, 0, :], rhs=kT[:, cols], start=True, stop=False)
            nc.tensor.matmul(score_of[n, b][:], lhsT=qT[:, n, 1, :], rhs=kT[:, cols], start=False, stop=True)

        def mask_scores(n, b):
            if not 0 <= n < N_TILES:
                return
            cols = slice(BANK * b, BANK * (b + 1))
            if b == 0:
                shifted_of[n] = work.tile([P, T], F32, name="shifted")
            nc.vector.scalar_tensor_tensor(out=shifted_of[n][:, cols], in0=mask_of[n][:, cols, 0], scalar=1.0,
                                           in1=score_of[n, b][:], op0=ALU.subtract, op1=ALU.add)

        def row_max(n):
            if not 0 <= n < N_TILES:
                return
            row_max_of[n] = small.tile([P, 1], F32, name="row_max")
            nc.vector.tensor_reduce(out=row_max_of[n][:], in_=shifted_of[n][:], axis=mybir.AxisListType.X, op=ALU.max)

        def exponent(n):
            if not 0 <= n < N_TILES:
                return
            neg_max = small.tile([P, 1], F32)
            nc.scalar.mul(out=neg_max[:], in_=row_max_of[n][:], mul=-GROW)
            e_of[n] = work.tile([P, T], BF16, name="e_sb")
            row_sum_of[n] = small.tile([P, 1], F32, name="row_sum")
            nc.scalar.activation(out=e_of[n][:], in_=shifted_of[n][:], func=ACT.Exp, bias=neg_max[:, 0:1],
                                 scale=GROW, accum_out=row_sum_of[n][:])
            inv_sum_of[n] = small.tile([P, 1], F32, name="inv_sum")
            nc.gpsimd.tensor_tensor(out=inv_sum_of[n][:], in0=row_sum_of[n][:], in1=minus_one[:], op=ALU.pow)

        def turn(n, c):
            if not 0 <= n < N_TILES:
                return
            if c % 2 == 0:
                turned_of[n, c // 2] = turn_psum.tile([P, 2, PACK, P], BF16, name="turned")
            for t in range(PACK):
                first = K_PASS * c + P * t
                nc.tensor.transpose(turned_of[n, c // 2][:, c % 2, t, :], e_of[n][:, first:first + P], ident[:])

        def regroup(n, h, on_vector):
            if not 0 <= n < N_TILES:
                return
            if h == 0:
                grouped_of[n] = work.tile([P, N_PASS, P, PACK], BF16, name="grouped", align_bytes=64)
            side_by_side = turned_of[n, h][:].rearrange("p c t r -> p c r t")
            if on_vector:
                nc.vector.tensor_copy(out=grouped_of[n][:, 2 * h:2 * h + 2], in_=side_by_side)
            else:
                nc.scalar.copy(out=grouped_of[n][:, 2 * h:2 * h + 2], in_=side_by_side)

        def quantise(n):
            if not 0 <= n < N_TILES:
                return
            codes_of[n] = work.tile([P, N_PASS, P], U32, name="e_codes", align_bytes=64)
            scales_of[n] = work.tile([P, N_PASS, P], U8, name="e_scales", align_bytes=64)
            nc.vector.quantize_mx(out=codes_of[n][:].rearrange("p c r -> p (c r)").bitcast(FP8X4),
                                  scales=scales_of[n][:].rearrange("p c r -> p (c r)"),
                                  in_=grouped_of[n][:].rearrange("p c r t -> p (c r t)"))

        def multiply(n):
            if not 0 <= n < N_TILES:
                return
            acc_of[n] = out_psum.tile([P, DV], F32, name="acc")
            for c in range(N_PASS):
                nc.tensor.matmul_mx(out=acc_of[n][:], lhsT=codes_of[n][:, c, :].bitcast(FP8X4),
                                    lhsT_scale=scales_of[n][:, c, :],
                                    rhs=v_codes[:, c, :].bitcast(FP8X4), rhs_scale=v_scales[:, c, :],
                                    start=(c == 0), stop=(c == N_PASS - 1))

        def finish(n):
            if not 0 <= n < N_TILES:
                return
            result = work.tile([P, DV], F32)
            nc.scalar.activation(out=result[:], in_=acc_of[n][:], func=ACT.Copy, scale=inv_sum_of[n][:, 0:1])
            nc.sync.dma_start(out=out_tiles[n], in_=result[:])

        def step(m):
            load_mask(m + MASKS_AHEAD)
            exponent(m - 1)
            regroup(m - 2, 0, False)
            regroup(m - 2, 1, False)
            for b in range(N_BANKS):
                mask_scores(m, b)
                scores(m + 1, b)
            quantise(m - 3)
            multiply(m - 3)
            finish(m - 3)
            for c in range(N_PASS):
                turn(m - 1, c)
            row_max(m)

        turn_keys(0)
        turn_keys(1)
        turn_queries(0)
        step(-1)
        for g in range(1, N_GROUPS):
            turn_queries(g)
        for m in range(0, 3):
            step(m)
        quantise_v()
        for m in range(3, N_TILES):
            step(m)

        last = N_TILES - 1
        exponent(last)
        quantise(last - 2)
        multiply(last - 2)
        finish(last - 2)
        regroup(last - 1, 0, True)
        regroup(last - 1, 1, True)
        for c in range(N_PASS):
            turn(last, c)
        quantise(last - 1)
        multiply(last - 1)
        regroup(last, 0, False)
        regroup(last, 1, True)
        finish(last - 1)
        quantise(last)
        multiply(last)
        finish(last)
